import numpy as np
import ml_dtypes


def mxq(x, axis, fmt="e4m3"):
    dtype, down = {"e4m3": (ml_dtypes.float8_e4m3fn, 7), "e5m2": (ml_dtypes.float8_e5m2, 14)}[fmt]
    v = np.moveaxis(np.asarray(x, np.float32).astype(ml_dtypes.bfloat16).astype(np.float64), axis, -1)
    blocks = v.reshape(v.shape[:-1] + (-1, 32))
    amax = np.abs(blocks).max(-1, keepdims=True)
    byte = np.maximum(np.where(amax > 0, np.frexp(amax)[1] - 1 + 127, 0) - down, 1)
    scale = np.exp2(byte - 127.0)
    codes = (blocks / scale).astype(np.float32).astype(dtype).astype(np.float64)
    return np.moveaxis((codes * scale).reshape(v.shape), -1, axis)


WIDE = False


def mx_kscale(k):
    if not WIDE:
        return np.ones(k)
    levels = np.array([20, -20, 10, -10, 0])
    a = np.random.permutation(np.resize(levels, k // 512 * 4)).reshape(k // 512, 4)
    idx = np.arange(k)
    return np.exp2(a[idx // 512, idx % 128 // 32])


BF16 = ml_dtypes.bfloat16


def bf(x):
    return np.asarray(x, np.float32).astype(BF16)


def f64(x):
    return np.asarray(x).astype(np.float64)


B, T, D, NH, HD, G, RD, F = 1, 1024, 1024, 8, 128, 2, 16, 4096
HKV = NH // G
C = NH * HD


def project(attn_out, v):
    y_g = f64(attn_out).transpose(0, 3, 1, 2, 4)
    v_t = f64(v).transpose(0, 2, 1, 3)
    vn = v_t / np.maximum(np.sqrt(np.sum(np.square(v_t), axis=-1, keepdims=True)), 1e-12)
    vn = vn[:, :, :, None, :]
    proj = np.sum(y_g * vn, axis=-1, keepdims=True) * vn
    return (y_g - proj).reshape(B, T, C)


def setup_inputs():
    s = mx_kscale(T)
    v = np.random.standard_normal((B, HKV, T, HD))
    a = 0.4 * np.random.standard_normal((B, HKV, G, T, HD)) + 0.4 * v[:, :, None]
    x = np.random.standard_normal((B, T, D)) * np.random.uniform(0.5, 2.0, (B, T, 1))
    wo = np.random.standard_normal((D, C)) / np.sqrt(C)
    attn_scale = 1.0 + 0.1 * np.random.standard_normal(D)
    g = np.random.standard_normal((B, T, D)) * np.exp2(np.random.randint(-12, 1, (B, T, 1))) / s[None, :, None]
    return {"attn_out": bf(a * s[None, None, None, :, None]),
            "v": bf(v),
            "x": bf(x),
            "wo": bf(wo),
            "attn_scale": bf(attn_scale),
            "grad_out": bf(g)}


def reference(attn_out, v, x, wo, attn_scale, grad_out):
    y = project(attn_out, v).reshape(B * T, C)
    g = f64(grad_out).reshape(B * T, D)
    p = mxq(g, 0, "e5m2").T @ mxq(y, 0, "e4m3")
    return f64(attn_scale)[:, None] * p

@@ -1,0 +1,272 @@
+from contextlib import ExitStack
+
+import concourse.mybir as mybir
+from concourse.masks import make_identity
+
+F32 = mybir.dt.float32
+BF16 = mybir.dt.bfloat16
+U32 = mybir.dt.uint32
+U8 = mybir.dt.uint8
+E4M3_X4 = mybir.dt.float8_e4m3fn_x4
+E5M2_X4 = mybir.dt.float8_e5m2_x4
+ALU = mybir.AluOpType
+ACT = mybir.ActivationFunctionType
+
+P = 128
+PACK = 4
+K_PASS = P * PACK
+TOKENS = 1024
+PASSES = TOKENS // K_PASS
+HEAD_DIM = 128
+KV_HEADS = 4
+GROUP = 2
+CHANNELS = 1024
+COLUMNS = KV_HEADS * GROUP * HEAD_DIM
+M_TILE = 128
+N_TILE = 512
+M_TILES = CHANNELS // M_TILE
+HALVES = COLUMNS // N_TILE
+Q_HEADS = N_TILE // HEAD_DIM
+KV_IN_HALF = Q_HEADS // GROUP
+NORM_FLOOR_SQUARED = 1e-24
+
+FLOPS = 2 * TOKENS * CHANNELS * COLUMNS
+BYTES = 2 * (TOKENS * COLUMNS + TOKENS * KV_HEADS * HEAD_DIM + TOKENS * CHANNELS + CHANNELS) + 4 * CHANNELS * COLUMNS
+
+
+def regrouped(grouped, rows):
+    return (
+        grouped.rearrange("p (c i) j -> p c j i", i=4),
+        rows.rearrange("p j (c i) -> p c j i", i=4),
+    )
+
+
+def tile_block_pb_kernel(tc, attn_out, v, x, wo, attn_scale, grad_out, out):
+    nc = tc.nc
+    CHUNKS = [(half, step) for half in range(HALVES) for step in range(PASSES)]
+    heads_q = attn_out.rearrange("b h g t d -> (b h g) t d")
+    heads_kv = v.rearrange("b h t d -> (b h) t d")
+    grad = grad_out.rearrange("b t d -> (b t) d")
+
+    with ExitStack() as stack:
+        keep = stack.enter_context(tc.tile_pool(name="keep", bufs=1))
+        work = stack.enter_context(tc.tile_pool(name="work", bufs=2))
+        stage = stack.enter_context(tc.tile_pool(name="stage", bufs=M_TILES))
+        psum = stack.enter_context(tc.psum_pool(name="psum", bufs=8))
+
+        a_sb = {}
+        v_sb = {}
+        g_sb = {}
+
+        def load_chunk(k):
+            half, step = CHUNKS[k]
+            tokens = slice(step * K_PASS, (step + 1) * K_PASS)
+            v_sb[k] = keep.tile([P, KV_IN_HALF, PACK * HEAD_DIM], BF16, name="v_sb%d" % k)
+            a_sb[k] = keep.tile([P, Q_HEADS, PACK * HEAD_DIM], BF16, name="a_sb%d" % k)
+            for h in range(KV_IN_HALF):
+                kv = half * KV_IN_HALF + h
+                nc.sync.dma_start(
+                    out=v_sb[k][:, h, :], in_=heads_kv[kv, tokens, :].rearrange("(p j) d -> p (j d)", j=PACK)
+                )
+                nc.sync.dma_start(
+                    out=a_sb[k][:, h * GROUP : (h + 1) * GROUP, :],
+                    in_=heads_q[kv * GROUP : (kv + 1) * GROUP, tokens, :].rearrange("g (p j) d -> p g (j d)", j=PACK),
+                )
+
+        def load_grad(step):
+            g_sb[step] = keep.tile([P, PACK, CHANNELS], BF16, name="g_sb%d" % step)
+            nc.sync.dma_start(
+                out=g_sb[step][:],
+                in_=grad[step * K_PASS : (step + 1) * K_PASS, :].rearrange("(p j) d -> p j d", j=PACK),
+            )
+
+        load_chunk(0)
+        load_chunk(1)
+        load_grad(0)
+        load_grad(1)
+        load_chunk(2)
+        load_chunk(3)
+
+        identity = keep.tile([P, P], BF16)
+        make_identity(nc, identity[:])
+        scale_rows = keep.tile([P, P], BF16)
+        nc.vector.memset(scale_rows[:], 0.0)
+        nc.sync.dma_start(out=scale_rows[0:M_TILES, :], in_=attn_scale.rearrange("(m p) -> m p", p=P))
+        scale_col = keep.tile([P, M_TILES], F32)
+
+        y_codes = keep.tile([P, PASSES, COLUMNS], U32, align_bytes=64)
+        y_scales = keep.tile([P, PASSES, COLUMNS], U8, align_bytes=64)
+        g_codes = keep.tile([P, PASSES, CHANNELS], U32, align_bytes=64)
+        g_scales = keep.tile([P, PASSES, CHANNELS], U8, align_bytes=64)
+
+        squares = keep.tile([P, KV_IN_HALF * PACK, HEAD_DIM], BF16)
+        products = {}
+        scaled_v = {}
+        norm2 = {}
+        minus_inverse = {}
+        dot = {}
+        minus_coef = {}
+        y_grouped = {}
+        g_grouped = {}
+        acc = {}
+
+        def head_slice(j):
+            return slice(j * HEAD_DIM, (j + 1) * HEAD_DIM)
+
+        def norms(k):
+            norm2[k] = keep.tile([P, KV_IN_HALF * PACK], F32, name="norm2_%d" % k)
+            for h in range(KV_IN_HALF):
+                for j in range(PACK):
+                    nc.scalar.activation(
+                        out=squares[:, h * PACK + j, :],
+                        in_=v_sb[k][:, h, head_slice(j)],
+                        func=ACT.Square,
+                        accum_out=norm2[k][:, h * PACK + j : h * PACK + j + 1],
+                    )
+
+        def regroup_grad(step):
+            for half in range(HALVES):
+                cols = slice(half * N_TILE, (half + 1) * N_TILE)
+                g_grouped[step, half] = keep.tile(
+                    [P, N_TILE, PACK], BF16, name="g_grouped%d_%d" % (step, half), align_bytes=64
+                )
+                dst, src = regrouped(g_grouped[step, half][:], g_sb[step][:, :, cols])
+                nc.scalar.copy(out=dst, in_=src)
+
+        def quantise_grad(step):
+            for half in range(HALVES):
+                cols = slice(half * N_TILE, (half + 1) * N_TILE)
+                nc.vector.quantize_mx(
+                    out=g_codes[:, step, cols].bitcast(E5M2_X4),
+                    scales=g_scales[:, step, cols],
+                    in_=g_grouped[step, half][:].rearrange("p w j -> p (w j)"),
+                )
+
+        def inverse_norms(k):
+            floored = work.tile([P, KV_IN_HALF * PACK], F32, name="floored")
+            nc.vector.tensor_scalar(
+                out=floored[:], in0=norm2[k][:], scalar1=NORM_FLOOR_SQUARED, scalar2=-1.0, op0=ALU.max, op1=ALU.mult
+            )
+            minus_inverse[k] = work.tile([P, KV_IN_HALF * PACK], F32, name="minus_inverse")
+            nc.vector.reciprocal(out=minus_inverse[k][:], in_=floored[:])
+
+        def dots(k):
+            products[k] = work.tile([P, Q_HEADS, PACK * HEAD_DIM], F32, name="products")
+            dot[k] = work.tile([P, Q_HEADS * PACK], F32, name="dot")
+            for h in range(KV_IN_HALF):
+                group = slice(h * GROUP, (h + 1) * GROUP)
+                nc.vector.tensor_tensor(
+                    out=products[k][:, group, :],
+                    in0=a_sb[k][:, group, :],
+                    in1=v_sb[k][:, h, :].unsqueeze(1).to_broadcast([P, GROUP, PACK * HEAD_DIM]),
+                    op=ALU.mult,
+                )
+            for h in range(KV_IN_HALF):
+                group = slice(h * GROUP, (h + 1) * GROUP)
+                nc.vector.tensor_reduce(
+                    out=dot[k][:, h * GROUP * PACK : (h + 1) * GROUP * PACK],
+                    in_=products[k][:, group, :].rearrange("p g (j d) -> p (g j) d", d=HEAD_DIM),
+                    axis=mybir.AxisListType.X,
+                    op=ALU.add,
+                )
+
+        def coefficients(k):
+            minus_coef[k] = work.tile([P, Q_HEADS * PACK], F32, name="minus_coef")
+            nc.vector.tensor_tensor(
+                out=minus_coef[k][:].rearrange("p (h g j) -> p h g j", g=GROUP, j=PACK),
+                in0=dot[k][:].rearrange("p (h g j) -> p h g j", g=GROUP, j=PACK),
+                in1=minus_inverse[k][:]
+                .rearrange("p (h j) -> p h j", j=PACK)
+                .unsqueeze(2)
+                .to_broadcast([P, KV_IN_HALF, GROUP, PACK]),
+                op=ALU.mult,
+            )
+
+        def scale_values(k):
+            scaled_v[k] = work.tile([P, Q_HEADS, PACK * HEAD_DIM], F32, name="scaled_v")
+            for q in range(Q_HEADS):
+                for j in range(PACK):
+                    nc.scalar.activation(
+                        out=scaled_v[k][:, q, head_slice(j)],
+                        in_=v_sb[k][:, q // GROUP, head_slice(j)],
+                        func=ACT.Copy,
+                        scale=minus_coef[k][:, q * PACK + j : q * PACK + j + 1],
+                    )
+
+        def project(k):
+            y_grouped[k] = work.tile([P, N_TILE, PACK], BF16, name="y_grouped", align_bytes=64)
+            for q in range(Q_HEADS):
+                nc.vector.tensor_tensor(
+                    out=y_grouped[k][:, q * HEAD_DIM : (q + 1) * HEAD_DIM, :].rearrange("p (c i) j -> p c j i", i=4),
+                    in0=a_sb[k][:, q, :].rearrange("p (j c i) -> p c j i", j=PACK, i=4),
+                    in1=scaled_v[k][:, q, :].rearrange("p (j c i) -> p c j i", j=PACK, i=4),
+                    op=ALU.add,
+                )
+
+        def quantise_y(k):
+            half, step = CHUNKS[k]
+            cols = slice(half * N_TILE, (half + 1) * N_TILE)
+            nc.vector.quantize_mx(
+                out=y_codes[:, step, cols].bitcast(E4M3_X4),
+                scales=y_scales[:, step, cols],
+                in_=y_grouped[k][:].rearrange("p w j -> p (w j)"),
+            )
+
+        def multiply(k):
+            half, step = CHUNKS[k]
+            cols = slice(half * N_TILE, (half + 1) * N_TILE)
+            for m in range(M_TILES):
+                rows = slice(m * M_TILE, (m + 1) * M_TILE)
+                if step == 0:
+                    acc[half, m] = psum.tile([P, N_TILE], F32, name="acc%d_%d" % (half, m), tag="bank")
+                nc.tensor.matmul_mx(
+                    out=acc[half, m][:],
+                    lhsT=g_codes[:, step, rows].bitcast(E5M2_X4),
+                    lhsT_scale=g_scales[:, step, rows],
+                    rhs=y_codes[:, step, cols].bitcast(E4M3_X4),
+                    rhs_scale=y_scales[:, step, cols],
+                    start=(step == 0),
+                    stop=(step == PASSES - 1),
+                )
+
+        def scale_and_store(half, both_engines):
+            for m in range(M_TILES):
+                result = stage.tile([P, N_TILE], F32, name="result")
+                gain = scale_col[:, m : m + 1]
+                if both_engines and m % 2 == 1:
+                    nc.vector.tensor_scalar_mul(out=result[:], in0=acc[half, m][:], scalar1=gain)
+                else:
+                    nc.scalar.activation(out=result[:], in_=acc[half, m][:], func=ACT.Copy, scale=gain)
+                nc.sync.dma_start(
+                    out=out[m * M_TILE : (m + 1) * M_TILE, half * N_TILE : (half + 1) * N_TILE], in_=result[:]
+                )
+
+        def finish(k):
+            half, step = CHUNKS[k]
+            if half == 0:
+                quantise_grad(step)
+            quantise_y(k)
+            if k == 0:
+                scale_t = psum.tile([P, P], BF16, name="scale_t", tag="bank")
+                nc.tensor.transpose(scale_t[:], scale_rows[:], identity[:])
+                nc.scalar.copy(out=scale_col[:], in_=scale_t[:, 0:M_TILES])
+            multiply(k)
+            if step == PASSES - 1:
+                scale_and_store(half, both_engines=(half == HALVES - 1))
+
+        norms(0)
+        norms(1)
+        for k in range(len(CHUNKS)):
+            dots(k)
+            inverse_norms(k)
+            coefficients(k)
+            scale_values(k)
+            if k < PASSES:
+                regroup_grad(k)
+            if k + 2 < len(CHUNKS):
+                norms(k + 2)
+            if k >= 1:
+                project(k - 1)
+                finish(k - 1)
+        project(len(CHUNKS) - 1)
+        finish(len(CHUNKS) - 1)

@@ -1,7 +1,7 @@
 from contextlib import ExitStack
 
 import concourse.mybir as mybir
-from concourse.masks import make_identity
+from concourse.masks import make_block_diagonal, make_identity
 
 F32 = mybir.dt.float32
 BF16 = mybir.dt.bfloat16
@@ -29,6 +29,12 @@ HALVES = COLUMNS // N_TILE
 Q_HEADS = N_TILE // HEAD_DIM
 KV_IN_HALF = Q_HEADS // GROUP
 NORM_FLOOR_SQUARED = 1e-24
+CHUNK_WIDTH = Q_HEADS * PACK * HEAD_DIM
+DOTS = Q_HEADS * PACK
+SLICES = CHUNK_WIDTH // P
+PARTS = P // DOTS
+VECTOR_SHARE = (4, 2)
+OPEN_GROUPS = 6
 
 FLOPS = 2 * TOKENS * CHANNELS * COLUMNS
 BYTES = 2 * (TOKENS * COLUMNS + TOKENS * KV_HEADS * HEAD_DIM + TOKENS * CHANNELS + CHANNELS) + 4 * CHANNELS * COLUMNS
@@ -51,8 +57,10 @@ def tile_block_pb_kernel(tc, attn_out, v, x, wo, attn_scale, grad_out, out):
     with ExitStack() as stack:
         keep = stack.enter_context(tc.tile_pool(name="keep", bufs=1))
         work = stack.enter_context(tc.tile_pool(name="work", bufs=2))
+        ahead = stack.enter_context(tc.tile_pool(name="ahead", bufs=3))
         stage = stack.enter_context(tc.tile_pool(name="stage", bufs=M_TILES))
-        psum = stack.enter_context(tc.psum_pool(name="psum", bufs=8))
+        psum = stack.enter_context(tc.psum_pool(name="psum", bufs=OPEN_GROUPS))
+        psum_dots = stack.enter_context(tc.psum_pool(name="psum_dots", bufs=2))
 
         a_sb = {}
         v_sb = {}
@@ -82,17 +90,22 @@ def tile_block_pb_kernel(tc, attn_out, v, x, wo, attn_scale, grad_out, out):
 
         load_chunk(0)
         load_chunk(1)
-        load_grad(0)
-        load_grad(1)
         load_chunk(2)
+        load_grad(0)
         load_chunk(3)
+        load_grad(1)
 
         identity = keep.tile([P, P], BF16)
         make_identity(nc, identity[:])
         scale_rows = keep.tile([P, P], BF16)
         nc.vector.memset(scale_rows[:], 0.0)
-        nc.sync.dma_start(out=scale_rows[0:M_TILES, :], in_=attn_scale.rearrange("(m p) -> m p", p=P))
+        nc.scalar.dma_start(out=scale_rows[0:M_TILES, :], in_=attn_scale.rearrange("(m p) -> m p", p=P))
         scale_col = keep.tile([P, M_TILES], F32)
+
+        identity_f32 = keep.tile([P, P], F32)
+        make_identity(nc, identity_f32[:])
+        block_ones = keep.tile([P, P], F32)
+        make_block_diagonal(nc, block_ones[:], PARTS)
 
         y_codes = keep.tile([P, PASSES, COLUMNS], U32, align_bytes=64)
         y_scales = keep.tile([P, PASSES, COLUMNS], U8, align_bytes=64)
@@ -105,6 +118,7 @@ def tile_block_pb_kernel(tc, attn_out, v, x, wo, attn_scale, grad_out, out):
         norm2 = {}
         minus_inverse = {}
         dot = {}
+        partial = {}
         minus_coef = {}
         y_grouped = {}
         g_grouped = {}
@@ -124,14 +138,22 @@ def tile_block_pb_kernel(tc, attn_out, v, x, wo, attn_scale, grad_out, out):
                         accum_out=norm2[k][:, h * PACK + j : h * PACK + j + 1],
                     )
 
-        def regroup_grad(step):
+        def regroup_grad(step, on_vector):
             for half in range(HALVES):
-                cols = slice(half * N_TILE, (half + 1) * N_TILE)
                 g_grouped[step, half] = keep.tile(
                     [P, N_TILE, PACK], BF16, name="g_grouped%d_%d" % (step, half), align_bytes=64
                 )
-                dst, src = regrouped(g_grouped[step, half][:], g_sb[step][:, :, cols])
-                nc.scalar.copy(out=dst, in_=src)
+                for piece in range(2):
+                    width = N_TILE // 2
+                    first = half * N_TILE + piece * width
+                    dst, src = regrouped(
+                        g_grouped[step, half][:, piece * width : (piece + 1) * width, :],
+                        g_sb[step][:, :, first : first + width],
+                    )
+                    if on_vector:
+                        nc.vector.tensor_copy(out=dst, in_=src)
+                    else:
+                        nc.scalar.copy(out=dst, in_=src)
 
         def quantise_grad(step):
             for half in range(HALVES):
@@ -150,31 +172,43 @@ def tile_block_pb_kernel(tc, attn_out, v, x, wo, attn_scale, grad_out, out):
             minus_inverse[k] = work.tile([P, KV_IN_HALF * PACK], F32, name="minus_inverse")
             nc.vector.reciprocal(out=minus_inverse[k][:], in_=floored[:])
 
-        def dots(k):
-            products[k] = work.tile([P, Q_HEADS, PACK * HEAD_DIM], F32, name="products")
-            dot[k] = work.tile([P, Q_HEADS * PACK], F32, name="dot")
+        def multiply_values(k):
+            products[k] = ahead.tile([P, CHUNK_WIDTH], F32, name="products")
             for h in range(KV_IN_HALF):
                 group = slice(h * GROUP, (h + 1) * GROUP)
                 nc.vector.tensor_tensor(
-                    out=products[k][:, group, :],
+                    out=products[k][:].rearrange("p (q c) -> p q c", q=Q_HEADS)[:, group, :],
                     in0=a_sb[k][:, group, :],
                     in1=v_sb[k][:, h, :].unsqueeze(1).to_broadcast([P, GROUP, PACK * HEAD_DIM]),
                     op=ALU.mult,
                 )
-            for h in range(KV_IN_HALF):
-                group = slice(h * GROUP, (h + 1) * GROUP)
-                nc.vector.tensor_reduce(
-                    out=dot[k][:, h * GROUP * PACK : (h + 1) * GROUP * PACK],
-                    in_=products[k][:, group, :].rearrange("p g (j d) -> p (g j) d", d=HEAD_DIM),
-                    axis=mybir.AxisListType.X,
-                    op=ALU.add,
+
+        def sum_products(k):
+            dot[k] = psum_dots.tile([P, P + DOTS], F32, name="dot", tag="dots")
+            for s in range(SLICES):
+                nc.tensor.matmul(
+                    out=dot[k][:, 0:P],
+                    lhsT=products[k][:, s:CHUNK_WIDTH:SLICES],
+                    rhs=identity_f32[:],
+                    is_transpose=True,
+                    start=(s == 0),
+                    stop=(s == SLICES - 1),
                 )
+            partial[k] = work.tile([P, P], F32, name="partial")
+            nc.scalar.copy(out=partial[k][:], in_=dot[k][:, 0:P])
+            nc.tensor.matmul(
+                out=dot[k][:, P : P + DOTS],
+                lhsT=partial[k][:],
+                rhs=block_ones[:, 0:P:PARTS],
+                start=True,
+                stop=True,
+            )
 
         def coefficients(k):
             minus_coef[k] = work.tile([P, Q_HEADS * PACK], F32, name="minus_coef")
             nc.vector.tensor_tensor(
                 out=minus_coef[k][:].rearrange("p (h g j) -> p h g j", g=GROUP, j=PACK),
-                in0=dot[k][:].rearrange("p (h g j) -> p h g j", g=GROUP, j=PACK),
+                in0=dot[k][:, P : P + DOTS].rearrange("p (h g j) -> p h g j", g=GROUP, j=PACK),
                 in1=minus_inverse[k][:]
                 .rearrange("p (h j) -> p h j", j=PACK)
                 .unsqueeze(2)
@@ -212,61 +246,77 @@ def tile_block_pb_kernel(tc, attn_out, v, x, wo, attn_scale, grad_out, out):
                 in_=y_grouped[k][:].rearrange("p w j -> p (w j)"),
             )
 
-        def multiply(k):
-            half, step = CHUNKS[k]
+        def one_pass(half, step, m):
             cols = slice(half * N_TILE, (half + 1) * N_TILE)
-            for m in range(M_TILES):
-                rows = slice(m * M_TILE, (m + 1) * M_TILE)
-                if step == 0:
-                    acc[half, m] = psum.tile([P, N_TILE], F32, name="acc%d_%d" % (half, m), tag="bank")
-                nc.tensor.matmul_mx(
-                    out=acc[half, m][:],
-                    lhsT=g_codes[:, step, rows].bitcast(E5M2_X4),
-                    lhsT_scale=g_scales[:, step, rows],
-                    rhs=y_codes[:, step, cols].bitcast(E4M3_X4),
-                    rhs_scale=y_scales[:, step, cols],
-                    start=(step == 0),
-                    stop=(step == PASSES - 1),
-                )
+            rows = slice(m * M_TILE, (m + 1) * M_TILE)
+            if step == 0:
+                acc[half, m] = psum.tile([P, N_TILE], F32, name="acc%d_%d" % (half, m), tag="bank")
+            nc.tensor.matmul_mx(
+                out=acc[half, m][:],
+                lhsT=g_codes[:, step, rows].bitcast(E5M2_X4),
+                lhsT_scale=g_scales[:, step, rows],
+                rhs=y_codes[:, step, cols].bitcast(E4M3_X4),
+                rhs_scale=y_scales[:, step, cols],
+                start=(step == 0),
+                stop=(step == PASSES - 1),
+            )
 
-        def scale_and_store(half, both_engines):
-            for m in range(M_TILES):
-                result = stage.tile([P, N_TILE], F32, name="result")
-                gain = scale_col[:, m : m + 1]
-                if both_engines and m % 2 == 1:
-                    nc.vector.tensor_scalar_mul(out=result[:], in0=acc[half, m][:], scalar1=gain)
-                else:
-                    nc.scalar.activation(out=result[:], in_=acc[half, m][:], func=ACT.Copy, scale=gain)
-                nc.sync.dma_start(
-                    out=out[m * M_TILE : (m + 1) * M_TILE, half * N_TILE : (half + 1) * N_TILE], in_=result[:]
-                )
+        def scale_and_store(half, m, on_vector):
+            result = stage.tile([P, N_TILE], F32, name="result")
+            gain = scale_col[:, m : m + 1]
+            if on_vector:
+                nc.vector.tensor_scalar_mul(out=result[:], in0=acc[half, m][:], scalar1=gain)
+            else:
+                nc.scalar.activation(out=result[:], in_=acc[half, m][:], func=ACT.Copy, scale=gain)
+            nc.sync.dma_start(
+                out=out[m * M_TILE : (m + 1) * M_TILE, half * N_TILE : (half + 1) * N_TILE], in_=result[:]
+            )
 
         def finish(k):
             half, step = CHUNKS[k]
             if half == 0:
                 quantise_grad(step)
-            quantise_y(k)
-            if k == 0:
-                scale_t = psum.tile([P, P], BF16, name="scale_t", tag="bank")
-                nc.tensor.transpose(scale_t[:], scale_rows[:], identity[:])
-                nc.scalar.copy(out=scale_col[:], in_=scale_t[:, 0:M_TILES])
-            multiply(k)
-            if step == PASSES - 1:
-                scale_and_store(half, both_engines=(half == HALVES - 1))
+            if step == 0:
+                for m in range(OPEN_GROUPS):
+                    one_pass(half, 0, m)
+            else:
+                for m in range(M_TILES):
+                    if m >= OPEN_GROUPS:
+                        one_pass(half, 0, m)
+                    one_pass(half, 1, m)
+                    scale_and_store(half, m, on_vector=(m % VECTOR_SHARE[half] == VECTOR_SHARE[half] - 1))
 
-        norms(0)
-        norms(1)
-        for k in range(len(CHUNKS)):
-            dots(k)
+        scale_t = psum_dots.tile([P, P], BF16, name="scale_t", tag="dots")
+        nc.tensor.transpose(scale_t[:], scale_rows[:], identity[:])
+        nc.scalar.copy(out=scale_col[:], in_=scale_t[:, 0:M_TILES])
+
+        def start_chunk(k):
+            multiply_values(k)
+            sum_products(k)
+
+        def coefficients_and_scaled_values(k):
             inverse_norms(k)
             coefficients(k)
             scale_values(k)
+
+        def begin(k):
+            norms(k)
+            start_chunk(k)
+
+        begin(0)
+        begin(1)
+        coefficients_and_scaled_values(0)
+        begin(2)
+        for k in range(len(CHUNKS)):
+            if k + 1 < len(CHUNKS):
+                inverse_norms(k + 1)
+                coefficients(k + 1)
+            project(k)
+            quantise_y(k)
+            if k + 1 < len(CHUNKS):
+                scale_values(k + 1)
+            if k + 3 < len(CHUNKS):
+                begin(k + 3)
             if k < PASSES:
-                regroup_grad(k)
-            if k + 2 < len(CHUNKS):
-                norms(k + 2)
-            if k >= 1:
-                project(k - 1)
-                finish(k - 1)
-        project(len(CHUNKS) - 1)
-        finish(len(CHUNKS) - 1)
+                regroup_grad(k, on_vector=(k == 1))
+            finish(k)

@@ -117,6 +117,7 @@ def tile_block_pb_kernel(tc, attn_out, v, x, wo, attn_scale, grad_out, out):
         scaled_v = {}
         norm2 = {}
         minus_inverse = {}
+        floored = {}
         dot = {}
         partial = {}
         minus_coef = {}
@@ -164,24 +165,26 @@ def tile_block_pb_kernel(tc, attn_out, v, x, wo, attn_scale, grad_out, out):
                     in_=g_grouped[step, half][:].rearrange("p w j -> p (w j)"),
                 )
 
-        def inverse_norms(k):
-            floored = work.tile([P, KV_IN_HALF * PACK], F32, name="floored")
+        def floor_norms(k):
+            floored[k] = work.tile([P, KV_IN_HALF * PACK], F32, name="floored")
             nc.vector.tensor_scalar(
-                out=floored[:], in0=norm2[k][:], scalar1=NORM_FLOOR_SQUARED, scalar2=-1.0, op0=ALU.max, op1=ALU.mult
+                out=floored[k][:], in0=norm2[k][:], scalar1=NORM_FLOOR_SQUARED, scalar2=-1.0, op0=ALU.max, op1=ALU.mult
             )
-            minus_inverse[k] = work.tile([P, KV_IN_HALF * PACK], F32, name="minus_inverse")
-            nc.vector.reciprocal(out=minus_inverse[k][:], in_=floored[:])
 
-        def multiply_values(k):
-            products[k] = ahead.tile([P, CHUNK_WIDTH], F32, name="products")
-            for h in range(KV_IN_HALF):
-                group = slice(h * GROUP, (h + 1) * GROUP)
-                nc.vector.tensor_tensor(
-                    out=products[k][:].rearrange("p (q c) -> p q c", q=Q_HEADS)[:, group, :],
-                    in0=a_sb[k][:, group, :],
-                    in1=v_sb[k][:, h, :].unsqueeze(1).to_broadcast([P, GROUP, PACK * HEAD_DIM]),
-                    op=ALU.mult,
-                )
+        def invert_norms(k):
+            minus_inverse[k] = work.tile([P, KV_IN_HALF * PACK], F32, name="minus_inverse")
+            nc.vector.reciprocal(out=minus_inverse[k][:], in_=floored[k][:])
+
+        def multiply_values(k, h):
+            if h == 0:
+                products[k] = ahead.tile([P, CHUNK_WIDTH], F32, name="products")
+            group = slice(h * GROUP, (h + 1) * GROUP)
+            nc.vector.tensor_tensor(
+                out=products[k][:].rearrange("p (q c) -> p q c", q=Q_HEADS)[:, group, :],
+                in0=a_sb[k][:, group, :],
+                in1=v_sb[k][:, h, :].unsqueeze(1).to_broadcast([P, GROUP, PACK * HEAD_DIM]),
+                op=ALU.mult,
+            )
 
         def sum_products(k):
             dot[k] = psum_dots.tile([P, P + DOTS], F32, name="dot", tag="dots")
@@ -227,24 +230,26 @@ def tile_block_pb_kernel(tc, attn_out, v, x, wo, attn_scale, grad_out, out):
                         scale=minus_coef[k][:, q * PACK + j : q * PACK + j + 1],
                     )
 
-        def project(k):
-            y_grouped[k] = work.tile([P, N_TILE, PACK], BF16, name="y_grouped", align_bytes=64)
-            for q in range(Q_HEADS):
-                nc.vector.tensor_tensor(
-                    out=y_grouped[k][:, q * HEAD_DIM : (q + 1) * HEAD_DIM, :].rearrange("p (c i) j -> p c j i", i=4),
-                    in0=a_sb[k][:, q, :].rearrange("p (j c i) -> p c j i", j=PACK, i=4),
-                    in1=scaled_v[k][:, q, :].rearrange("p (j c i) -> p c j i", j=PACK, i=4),
-                    op=ALU.add,
-                )
+        def project(k, q):
+            if q == 0:
+                y_grouped[k] = work.tile([P, N_TILE, PACK], BF16, name="y_grouped", align_bytes=64)
+            nc.vector.tensor_tensor(
+                out=y_grouped[k][:, q * HEAD_DIM : (q + 1) * HEAD_DIM, :].rearrange("p (c i) j -> p c j i", i=4),
+                in0=a_sb[k][:, q, :].rearrange("p (j c i) -> p c j i", j=PACK, i=4),
+                in1=scaled_v[k][:, q, :].rearrange("p (j c i) -> p c j i", j=PACK, i=4),
+                op=ALU.add,
+            )
 
         def quantise_y(k):
             half, step = CHUNKS[k]
-            cols = slice(half * N_TILE, (half + 1) * N_TILE)
-            nc.vector.quantize_mx(
-                out=y_codes[:, step, cols].bitcast(E4M3_X4),
-                scales=y_scales[:, step, cols],
-                in_=y_grouped[k][:].rearrange("p w j -> p (w j)"),
-            )
+            width = GROUP * HEAD_DIM
+            for h in range(KV_IN_HALF):
+                cols = slice(half * N_TILE + h * width, half * N_TILE + (h + 1) * width)
+                nc.vector.quantize_mx(
+                    out=y_codes[:, step, cols].bitcast(E4M3_X4),
+                    scales=y_scales[:, step, cols],
+                    in_=y_grouped[k][:, h * width : (h + 1) * width, :].rearrange("p w j -> p (w j)"),
+                )
 
         def one_pass(half, step, m):
             cols = slice(half * N_TILE, (half + 1) * N_TILE)
@@ -290,30 +295,36 @@ def tile_block_pb_kernel(tc, attn_out, v, x, wo, attn_scale, grad_out, out):
         nc.tensor.transpose(scale_t[:], scale_rows[:], identity[:])
         nc.scalar.copy(out=scale_col[:], in_=scale_t[:, 0:M_TILES])
 
-        def start_chunk(k):
-            multiply_values(k)
-            sum_products(k)
-
-        def coefficients_and_scaled_values(k):
-            inverse_norms(k)
-            coefficients(k)
-            scale_values(k)
-
         def begin(k):
             norms(k)
-            start_chunk(k)
+            multiply_values(k, 0)
+            multiply_values(k, 1)
+            sum_products(k)
 
         begin(0)
-        begin(1)
-        coefficients_and_scaled_values(0)
+        norms(1)
+        floor_norms(0)
+        multiply_values(1, 0)
+        invert_norms(0)
+        multiply_values(1, 1)
+        sum_products(1)
+        coefficients(0)
+        scale_values(0)
         begin(2)
         for k in range(len(CHUNKS)):
-            if k + 1 < len(CHUNKS):
-                inverse_norms(k + 1)
+            more = k + 1 < len(CHUNKS)
+            if more:
+                floor_norms(k + 1)
+            project(k, 0)
+            if more:
+                invert_norms(k + 1)
+            project(k, 1)
+            if more:
                 coefficients(k + 1)
-            project(k)
+            project(k, 2)
+            project(k, 3)
             quantise_y(k)
-            if k + 1 < len(CHUNKS):
+            if more:
                 scale_values(k + 1)
             if k + 3 < len(CHUNKS):
                 begin(k + 3)

@@ -33,7 +33,6 @@ CHUNK_WIDTH = Q_HEADS * PACK * HEAD_DIM
 DOTS = Q_HEADS * PACK
 SLICES = CHUNK_WIDTH // P
 PARTS = P // DOTS
-VECTOR_SHARE = (4, 2)
 OPEN_GROUPS = 6
 
 FLOPS = 2 * TOKENS * CHANNELS * COLUMNS
@@ -277,20 +276,6 @@ def tile_block_pb_kernel(tc, attn_out, v, x, wo, attn_scale, grad_out, out):
                 out=out[m * M_TILE : (m + 1) * M_TILE, half * N_TILE : (half + 1) * N_TILE], in_=result[:]
             )
 
-        def finish(k):
-            half, step = CHUNKS[k]
-            if half == 0:
-                quantise_grad(step)
-            if step == 0:
-                for m in range(OPEN_GROUPS):
-                    one_pass(half, 0, m)
-            else:
-                for m in range(M_TILES):
-                    if m >= OPEN_GROUPS:
-                        one_pass(half, 0, m)
-                    one_pass(half, 1, m)
-                    scale_and_store(half, m, on_vector=(m % VECTOR_SHARE[half] == VECTOR_SHARE[half] - 1))
-
         scale_t = psum_dots.tile([P, P], BF16, name="scale_t", tag="dots")
         nc.tensor.transpose(scale_t[:], scale_rows[:], identity[:])
         nc.scalar.copy(out=scale_col[:], in_=scale_t[:, 0:M_TILES])
@@ -326,8 +311,29 @@ def tile_block_pb_kernel(tc, attn_out, v, x, wo, attn_scale, grad_out, out):
             quantise_y(k)
             if more:
                 scale_values(k + 1)
+            if k == 2:
+                for m in range(M_TILES - OPEN_GROUPS):
+                    scale_and_store(0, m, on_vector=False)
+                for m in range(OPEN_GROUPS, M_TILES):
+                    one_pass(0, 0, m)
+                    one_pass(0, 1, m)
+                for m in range(M_TILES - OPEN_GROUPS, M_TILES):
+                    scale_and_store(0, m, on_vector=False)
             if k + 3 < len(CHUNKS):
                 begin(k + 3)
             if k < PASSES:
                 regroup_grad(k, on_vector=(k == 1))
-            finish(k)
+                quantise_grad(k)
+            if k == 1:
+                for m in range(OPEN_GROUPS):
+                    one_pass(0, 0, m)
+                    one_pass(0, 1, m)
+            if k == 2:
+                for m in range(OPEN_GROUPS):
+                    one_pass(1, 0, m)
+            if k == 3:
+                for m in range(M_TILES):
+                    if m >= OPEN_GROUPS:
+                        one_pass(1, 0, m)
+                    one_pass(1, 1, m)
+                    scale_and_store(1, m, on_vector=(m % 2 == 1))

@@ -177,20 +177,21 @@ def tile_block_pb_kernel(tc, attn_out, v, x, wo, attn_scale, grad_out, out):
         def multiply_values(k, h):
             if h == 0:
                 products[k] = ahead.tile([P, CHUNK_WIDTH], F32, name="products")
-            group = slice(h * GROUP, (h + 1) * GROUP)
-            nc.vector.tensor_tensor(
-                out=products[k][:].rearrange("p (q c) -> p q c", q=Q_HEADS)[:, group, :],
-                in0=a_sb[k][:, group, :],
-                in1=v_sb[k][:, h, :].unsqueeze(1).to_broadcast([P, GROUP, PACK * HEAD_DIM]),
-                op=ALU.mult,
-            )
+            by_head = products[k][:].rearrange("p (s q j r) -> p q j s r", q=Q_HEADS, j=PACK, r=PARTS)
+            for q in range(h * GROUP, (h + 1) * GROUP):
+                nc.vector.tensor_tensor(
+                    out=by_head[:, q],
+                    in0=a_sb[k][:, q, :].rearrange("p (j s r) -> p j s r", j=PACK, r=PARTS),
+                    in1=v_sb[k][:, h, :].rearrange("p (j s r) -> p j s r", j=PACK, r=PARTS),
+                    op=ALU.mult,
+                )
 
         def sum_products(k):
             dot[k] = psum_dots.tile([P, P + DOTS], F32, name="dot", tag="dots")
             for s in range(SLICES):
                 nc.tensor.matmul(
                     out=dot[k][:, 0:P],
-                    lhsT=products[k][:, s:CHUNK_WIDTH:SLICES],
+                    lhsT=products[k][:, s * P : (s + 1) * P],
                     rhs=identity_f32[:],
                     is_transpose=True,
                     start=(s == 0),

@@ -178,13 +178,16 @@ def tile_block_pb_kernel(tc, attn_out, v, x, wo, attn_scale, grad_out, out):
             if h == 0:
                 products[k] = ahead.tile([P, CHUNK_WIDTH], F32, name="products")
             by_head = products[k][:].rearrange("p (s q j r) -> p q j s r", q=Q_HEADS, j=PACK, r=PARTS)
-            for q in range(h * GROUP, (h + 1) * GROUP):
-                nc.vector.tensor_tensor(
-                    out=by_head[:, q],
-                    in0=a_sb[k][:, q, :].rearrange("p (j s r) -> p j s r", j=PACK, r=PARTS),
-                    in1=v_sb[k][:, h, :].rearrange("p (j s r) -> p j s r", j=PACK, r=PARTS),
-                    op=ALU.mult,
-                )
+            group = slice(h * GROUP, (h + 1) * GROUP)
+            nc.vector.tensor_tensor(
+                out=by_head[:, group],
+                in0=a_sb[k][:, group, :].rearrange("p g (j s r) -> p g j s r", j=PACK, r=PARTS),
+                in1=v_sb[k][:, h, :]
+                .rearrange("p (j s r) -> p j s r", j=PACK, r=PARTS)
+                .unsqueeze(1)
+                .to_broadcast([P, GROUP, PACK, SLICES, PARTS]),
+                op=ALU.mult,
+            )
 
         def sum_products(k):
             dot[k] = psum_dots.tile([P, P + DOTS], F32, name="dot", tag="dots")

@@ -312,6 +312,16 @@ def tile_block_pb_kernel(tc, attn_out, v, x, wo, attn_scale, grad_out, out):
                 coefficients(k + 1)
             project(k, 2)
             project(k, 3)
+            if not more:
+                warm = psum_dots.tile([P, N_TILE], F32, name="warm", tag="dots")
+                for q in range(Q_HEADS):
+                    nc.tensor.matmul(
+                        out=warm[:],
+                        lhsT=identity[:],
+                        rhs=y_grouped[k][:, q * HEAD_DIM : (q + 1) * HEAD_DIM, :].rearrange("p w j -> p (w j)"),
+                        start=True,
+                        stop=True,
+                    )
             quantise_y(k)
             if more:
                 scale_values(k + 1)

@@ -57,7 +57,7 @@ def tile_block_pb_kernel(tc, attn_out, v, x, wo, attn_scale, grad_out, out):
         keep = stack.enter_context(tc.tile_pool(name="keep", bufs=1))
         work = stack.enter_context(tc.tile_pool(name="work", bufs=2))
         ahead = stack.enter_context(tc.tile_pool(name="ahead", bufs=3))
-        stage = stack.enter_context(tc.tile_pool(name="stage", bufs=M_TILES))
+        stage = stack.enter_context(tc.tile_pool(name="stage", bufs=HALVES * M_TILES))
         psum = stack.enter_context(tc.psum_pool(name="psum", bufs=OPEN_GROUPS))
         psum_dots = stack.enter_context(tc.psum_pool(name="psum_dots", bufs=2))
 

@@ -166,7 +166,7 @@ def tile_block_pb_kernel(tc, attn_out, v, x, wo, attn_scale, grad_out, out):
 
         def floor_norms(k):
             floored[k] = work.tile([P, KV_IN_HALF * PACK], F32, name="floored")
-            nc.vector.tensor_scalar(
+            nc.gpsimd.tensor_scalar(
                 out=floored[k][:], in0=norm2[k][:], scalar1=NORM_FLOOR_SQUARED, scalar2=-1.0, op0=ALU.max, op1=ALU.mult
             )
 

from contextlib import ExitStack

import concourse.mybir as mybir
from concourse.masks import make_block_diagonal, make_identity

F32 = mybir.dt.float32
BF16 = mybir.dt.bfloat16
U32 = mybir.dt.uint32
U8 = mybir.dt.uint8
E4M3_X4 = mybir.dt.float8_e4m3fn_x4
E5M2_X4 = mybir.dt.float8_e5m2_x4
ALU = mybir.AluOpType
ACT = mybir.ActivationFunctionType

P = 128
PACK = 4
K_PASS = P * PACK
TOKENS = 1024
PASSES = TOKENS // K_PASS
HEAD_DIM = 128
KV_HEADS = 4
GROUP = 2
CHANNELS = 1024
COLUMNS = KV_HEADS * GROUP * HEAD_DIM
M_TILE = 128
N_TILE = 512
M_TILES = CHANNELS // M_TILE
HALVES = COLUMNS // N_TILE
Q_HEADS = N_TILE // HEAD_DIM
KV_IN_HALF = Q_HEADS // GROUP
NORM_FLOOR_SQUARED = 1e-24
CHUNK_WIDTH = Q_HEADS * PACK * HEAD_DIM
DOTS = Q_HEADS * PACK
SLICES = CHUNK_WIDTH // P
PARTS = P // DOTS
OPEN_GROUPS = 6

FLOPS = 2 * TOKENS * CHANNELS * COLUMNS
BYTES = 2 * (TOKENS * COLUMNS + TOKENS * KV_HEADS * HEAD_DIM + TOKENS * CHANNELS + CHANNELS) + 4 * CHANNELS * COLUMNS


def regrouped(grouped, rows):
    return (
        grouped.rearrange("p (c i) j -> p c j i", i=4),
        rows.rearrange("p j (c i) -> p c j i", i=4),
    )


def tile_block_pb_kernel(tc, attn_out, v, x, wo, attn_scale, grad_out, out):
    nc = tc.nc
    CHUNKS = [(half, step) for half in range(HALVES) for step in range(PASSES)]
    heads_q = attn_out.rearrange("b h g t d -> (b h g) t d")
    heads_kv = v.rearrange("b h t d -> (b h) t d")
    grad = grad_out.rearrange("b t d -> (b t) d")

    with ExitStack() as stack:
        keep = stack.enter_context(tc.tile_pool(name="keep", bufs=1))
        work = stack.enter_context(tc.tile_pool(name="work", bufs=2))
        ahead = stack.enter_context(tc.tile_pool(name="ahead", bufs=3))
        stage = stack.enter_context(tc.tile_pool(name="stage", bufs=HALVES * M_TILES))
        psum = stack.enter_context(tc.psum_pool(name="psum", bufs=OPEN_GROUPS))
        psum_dots = stack.enter_context(tc.psum_pool(name="psum_dots", bufs=2))

        a_sb = {}
        v_sb = {}
        g_sb = {}

        def load_chunk(k):
            half, step = CHUNKS[k]
            tokens = slice(step * K_PASS, (step + 1) * K_PASS)
            v_sb[k] = keep.tile([P, KV_IN_HALF, PACK * HEAD_DIM], BF16, name="v_sb%d" % k)
            a_sb[k] = keep.tile([P, Q_HEADS, PACK * HEAD_DIM], BF16, name="a_sb%d" % k)
            for h in range(KV_IN_HALF):
                kv = half * KV_IN_HALF + h
                nc.sync.dma_start(
                    out=v_sb[k][:, h, :], in_=heads_kv[kv, tokens, :].rearrange("(p j) d -> p (j d)", j=PACK)
                )
                nc.sync.dma_start(
                    out=a_sb[k][:, h * GROUP : (h + 1) * GROUP, :],
                    in_=heads_q[kv * GROUP : (kv + 1) * GROUP, tokens, :].rearrange("g (p j) d -> p g (j d)", j=PACK),
                )

        def load_grad(step):
            g_sb[step] = keep.tile([P, PACK, CHANNELS], BF16, name="g_sb%d" % step)
            nc.sync.dma_start(
                out=g_sb[step][:],
                in_=grad[step * K_PASS : (step + 1) * K_PASS, :].rearrange("(p j) d -> p j d", j=PACK),
            )

        load_chunk(0)
        load_chunk(1)
        load_chunk(2)
        load_grad(0)
        load_chunk(3)
        load_grad(1)

        identity = keep.tile([P, P], BF16)
        make_identity(nc, identity[:])
        scale_rows = keep.tile([P, P], BF16)
        nc.vector.memset(scale_rows[:], 0.0)
        nc.scalar.dma_start(out=scale_rows[0:M_TILES, :], in_=attn_scale.rearrange("(m p) -> m p", p=P))
        scale_col = keep.tile([P, M_TILES], F32)

        identity_f32 = keep.tile([P, P], F32)
        make_identity(nc, identity_f32[:])
        block_ones = keep.tile([P, P], F32)
        make_block_diagonal(nc, block_ones[:], PARTS)

        y_codes = keep.tile([P, PASSES, COLUMNS], U32, align_bytes=64)
        y_scales = keep.tile([P, PASSES, COLUMNS], U8, align_bytes=64)
        g_codes = keep.tile([P, PASSES, CHANNELS], U32, align_bytes=64)
        g_scales = keep.tile([P, PASSES, CHANNELS], U8, align_bytes=64)

        squares = keep.tile([P, KV_IN_HALF * PACK, HEAD_DIM], BF16)
        products = {}
        scaled_v = {}
        norm2 = {}
        minus_inverse = {}
        floored = {}
        dot = {}
        partial = {}
        minus_coef = {}
        y_grouped = {}
        g_grouped = {}
        acc = {}

        def head_slice(j):
            return slice(j * HEAD_DIM, (j + 1) * HEAD_DIM)

        def norms(k):
            norm2[k] = keep.tile([P, KV_IN_HALF * PACK], F32, name="norm2_%d" % k)
            for h in range(KV_IN_HALF):
                for j in range(PACK):
                    nc.scalar.activation(
                        out=squares[:, h * PACK + j, :],
                        in_=v_sb[k][:, h, head_slice(j)],
                        func=ACT.Square,
                        accum_out=norm2[k][:, h * PACK + j : h * PACK + j + 1],
                    )

        def regroup_grad(step, on_vector):
            for half in range(HALVES):
                g_grouped[step, half] = keep.tile(
                    [P, N_TILE, PACK], BF16, name="g_grouped%d_%d" % (step, half), align_bytes=64
                )
                for piece in range(2):
                    width = N_TILE // 2
                    first = half * N_TILE + piece * width
                    dst, src = regrouped(
                        g_grouped[step, half][:, piece * width : (piece + 1) * width, :],
                        g_sb[step][:, :, first : first + width],
                    )
                    if on_vector:
                        nc.vector.tensor_copy(out=dst, in_=src)
                    else:
                        nc.scalar.copy(out=dst, in_=src)

        def quantise_grad(step):
            for half in range(HALVES):
                cols = slice(half * N_TILE, (half + 1) * N_TILE)
                nc.vector.quantize_mx(
                    out=g_codes[:, step, cols].bitcast(E5M2_X4),
                    scales=g_scales[:, step, cols],
                    in_=g_grouped[step, half][:].rearrange("p w j -> p (w j)"),
                )

        def floor_norms(k):
            floored[k] = work.tile([P, KV_IN_HALF * PACK], F32, name="floored")
            nc.gpsimd.tensor_scalar(
                out=floored[k][:], in0=norm2[k][:], scalar1=NORM_FLOOR_SQUARED, scalar2=-1.0, op0=ALU.max, op1=ALU.mult
            )

        def invert_norms(k):
            minus_inverse[k] = work.tile([P, KV_IN_HALF * PACK], F32, name="minus_inverse")
            nc.vector.reciprocal(out=minus_inverse[k][:], in_=floored[k][:])

        def multiply_values(k, h):
            if h == 0:
                products[k] = ahead.tile([P, CHUNK_WIDTH], F32, name="products")
            by_head = products[k][:].rearrange("p (s q j r) -> p q j s r", q=Q_HEADS, j=PACK, r=PARTS)
            group = slice(h * GROUP, (h + 1) * GROUP)
            nc.vector.tensor_tensor(
                out=by_head[:, group],
                in0=a_sb[k][:, group, :].rearrange("p g (j s r) -> p g j s r", j=PACK, r=PARTS),
                in1=v_sb[k][:, h, :]
                .rearrange("p (j s r) -> p j s r", j=PACK, r=PARTS)
                .unsqueeze(1)
                .to_broadcast([P, GROUP, PACK, SLICES, PARTS]),
                op=ALU.mult,
            )

        def sum_products(k):
            dot[k] = psum_dots.tile([P, P + DOTS], F32, name="dot", tag="dots")
            for s in range(SLICES):
                nc.tensor.matmul(
                    out=dot[k][:, 0:P],
                    lhsT=products[k][:, s * P : (s + 1) * P],
                    rhs=identity_f32[:],
                    is_transpose=True,
                    start=(s == 0),
                    stop=(s == SLICES - 1),
                )
            partial[k] = work.tile([P, P], F32, name="partial")
            nc.scalar.copy(out=partial[k][:], in_=dot[k][:, 0:P])
            nc.tensor.matmul(
                out=dot[k][:, P : P + DOTS],
                lhsT=partial[k][:],
                rhs=block_ones[:, 0:P:PARTS],
                start=True,
                stop=True,
            )

        def coefficients(k):
            minus_coef[k] = work.tile([P, Q_HEADS * PACK], F32, name="minus_coef")
            nc.vector.tensor_tensor(
                out=minus_coef[k][:].rearrange("p (h g j) -> p h g j", g=GROUP, j=PACK),
                in0=dot[k][:, P : P + DOTS].rearrange("p (h g j) -> p h g j", g=GROUP, j=PACK),
                in1=minus_inverse[k][:]
                .rearrange("p (h j) -> p h j", j=PACK)
                .unsqueeze(2)
                .to_broadcast([P, KV_IN_HALF, GROUP, PACK]),
                op=ALU.mult,
            )

        def scale_values(k):
            scaled_v[k] = work.tile([P, Q_HEADS, PACK * HEAD_DIM], F32, name="scaled_v")
            for q in range(Q_HEADS):
                for j in range(PACK):
                    nc.scalar.activation(
                        out=scaled_v[k][:, q, head_slice(j)],
                        in_=v_sb[k][:, q // GROUP, head_slice(j)],
                        func=ACT.Copy,
                        scale=minus_coef[k][:, q * PACK + j : q * PACK + j + 1],
                    )

        def project(k, q):
            if q == 0:
                y_grouped[k] = work.tile([P, N_TILE, PACK], BF16, name="y_grouped", align_bytes=64)
            nc.vector.tensor_tensor(
                out=y_grouped[k][:, q * HEAD_DIM : (q + 1) * HEAD_DIM, :].rearrange("p (c i) j -> p c j i", i=4),
                in0=a_sb[k][:, q, :].rearrange("p (j c i) -> p c j i", j=PACK, i=4),
                in1=scaled_v[k][:, q, :].rearrange("p (j c i) -> p c j i", j=PACK, i=4),
                op=ALU.add,
            )

        def quantise_y(k):
            half, step = CHUNKS[k]
            width = GROUP * HEAD_DIM
            for h in range(KV_IN_HALF):
                cols = slice(half * N_TILE + h * width, half * N_TILE + (h + 1) * width)
                nc.vector.quantize_mx(
                    out=y_codes[:, step, cols].bitcast(E4M3_X4),
                    scales=y_scales[:, step, cols],
                    in_=y_grouped[k][:, h * width : (h + 1) * width, :].rearrange("p w j -> p (w j)"),
                )

        def one_pass(half, step, m):
            cols = slice(half * N_TILE, (half + 1) * N_TILE)
            rows = slice(m * M_TILE, (m + 1) * M_TILE)
            if step == 0:
                acc[half, m] = psum.tile([P, N_TILE], F32, name="acc%d_%d" % (half, m), tag="bank")
            nc.tensor.matmul_mx(
                out=acc[half, m][:],
                lhsT=g_codes[:, step, rows].bitcast(E5M2_X4),
                lhsT_scale=g_scales[:, step, rows],
                rhs=y_codes[:, step, cols].bitcast(E4M3_X4),
                rhs_scale=y_scales[:, step, cols],
                start=(step == 0),
                stop=(step == PASSES - 1),
            )

        def scale_and_store(half, m, on_vector):
            result = stage.tile([P, N_TILE], F32, name="result")
            gain = scale_col[:, m : m + 1]
            if on_vector:
                nc.vector.tensor_scalar_mul(out=result[:], in0=acc[half, m][:], scalar1=gain)
            else:
                nc.scalar.activation(out=result[:], in_=acc[half, m][:], func=ACT.Copy, scale=gain)
            nc.sync.dma_start(
                out=out[m * M_TILE : (m + 1) * M_TILE, half * N_TILE : (half + 1) * N_TILE], in_=result[:]
            )

        scale_t = psum_dots.tile([P, P], BF16, name="scale_t", tag="dots")
        nc.tensor.transpose(scale_t[:], scale_rows[:], identity[:])
        nc.scalar.copy(out=scale_col[:], in_=scale_t[:, 0:M_TILES])

        def begin(k):
            norms(k)
            multiply_values(k, 0)
            multiply_values(k, 1)
            sum_products(k)

        begin(0)
        norms(1)
        floor_norms(0)
        multiply_values(1, 0)
        invert_norms(0)
        multiply_values(1, 1)
        sum_products(1)
        coefficients(0)
        scale_values(0)
        begin(2)
        for k in range(len(CHUNKS)):
            more = k + 1 < len(CHUNKS)
            if more:
                floor_norms(k + 1)
            project(k, 0)
            if more:
                invert_norms(k + 1)
            project(k, 1)
            if more:
                coefficients(k + 1)
            project(k, 2)
            project(k, 3)
            if not more:
                warm = psum_dots.tile([P, N_TILE], F32, name="warm", tag="dots")
                for q in range(Q_HEADS):
                    nc.tensor.matmul(
                        out=warm[:],
                        lhsT=identity[:],
                        rhs=y_grouped[k][:, q * HEAD_DIM : (q + 1) * HEAD_DIM, :].rearrange("p w j -> p (w j)"),
                        start=True,
                        stop=True,
                    )
            quantise_y(k)
            if more:
                scale_values(k + 1)
            if k == 2:
                for m in range(M_TILES - OPEN_GROUPS):
                    scale_and_store(0, m, on_vector=False)
                for m in range(OPEN_GROUPS, M_TILES):
                    one_pass(0, 0, m)
                    one_pass(0, 1, m)
                for m in range(M_TILES - OPEN_GROUPS, M_TILES):
                    scale_and_store(0, m, on_vector=False)
            if k + 3 < len(CHUNKS):
                begin(k + 3)
            if k < PASSES:
                regroup_grad(k, on_vector=(k == 1))
                quantise_grad(k)
            if k == 1:
                for m in range(OPEN_GROUPS):
                    one_pass(0, 0, m)
                    one_pass(0, 1, m)
            if k == 2:
                for m in range(OPEN_GROUPS):
                    one_pass(1, 0, m)
            if k == 3:
                for m in range(M_TILES):
                    if m >= OPEN_GROUPS:
                        one_pass(1, 0, m)
                    one_pass(1, 1, m)
                    scale_and_store(1, m, on_vector=(m % 2 == 1))
